import numpy as np
import ml_dtypes


def mxq(x, axis, fmt="e4m3"):
    dtype, down = {"e4m3": (ml_dtypes.float8_e4m3fn, 7), "e5m2": (ml_dtypes.float8_e5m2, 14)}[fmt]
    v = np.moveaxis(np.asarray(x, np.float32).astype(ml_dtypes.bfloat16).astype(np.float64), axis, -1)
    blocks = v.reshape(v.shape[:-1] + (-1, 32))
    amax = np.abs(blocks).max(-1, keepdims=True)
    byte = np.maximum(np.where(amax > 0, np.frexp(amax)[1] - 1 + 127, 0) - down, 1)
    scale = np.exp2(byte - 127.0)
    codes = (blocks / scale).astype(np.float32).astype(dtype).astype(np.float64)
    return np.moveaxis((codes * scale).reshape(v.shape), -1, axis)


WIDE = False


def mx_kscale(k):
    if not WIDE:
        return np.ones(k)
    levels = np.array([20, -20, 10, -10, 0])
    a = np.random.permutation(np.resize(levels, k // 512 * 4)).reshape(k // 512, 4)
    idx = np.arange(k)
    return np.exp2(a[idx // 512, idx % 128 // 32])


BF16 = ml_dtypes.bfloat16


def bf(x):
    return np.asarray(x, np.float32).astype(BF16)


def f64(x):
    return np.asarray(x).astype(np.float64)


BATCH, WIDTH = 8192, 512


def setup_inputs():
    s = mx_kscale(BATCH)[:, None]
    x = np.random.standard_normal((BATCH, WIDTH)) * s
    W = np.random.standard_normal((WIDTH, WIDTH)) * (0.5 / np.sqrt(WIDTH))
    g = np.random.standard_normal((BATCH, WIDTH)) * np.exp2(np.random.randint(-12, 1, (BATCH, 1))) * 0.1 / s
    return {'x': bf(x), 'W': bf(W), 'grad_out': bf(g)}


def _adjoint_permuted_sum(M):
    return (
        2.0 * M.T
        + np.rot90(M, k=3)
        + np.rot90(M, k=2)
        + np.rot90(M, k=1)
        + M[::-1, :]
        + M[:, ::-1]
        + M.T[::-1, ::-1]
        + np.roll(M, shift=-1, axis=0)
        + np.roll(M, shift=-1, axis=1)
    )


def reference(x, W, grad_out):
    M = mxq(f64(x), 0, 'e4m3').T @ mxq(f64(grad_out), 0, 'e5m2')
    return _adjoint_permuted_sum(M)

@@ -1,0 +1,170 @@
+from contextlib import ExitStack
+
+import concourse.bass as bass
+import concourse.mybir as mybir
+import concourse.tile as tile
+from concourse.masks import make_identity
+
+F32 = mybir.dt.float32
+BF16 = mybir.dt.bfloat16
+U32 = mybir.dt.uint32
+U8 = mybir.dt.uint8
+E4 = mybir.dt.float8_e4m3fn_x4
+E5 = mybir.dt.float8_e5m2_x4
+ALU = mybir.AluOpType
+
+P = 128
+PACK = 4
+K_PASS = P * PACK
+TOKENS = 8192
+WIDTH = 512
+PASSES = TOKENS // K_PASS
+NT = WIDTH // P
+
+FLOPS = 2 * TOKENS * WIDTH * WIDTH
+BYTES = 2 * TOKENS * WIDTH * 2 + WIDTH * WIDTH * 4
+
+
+def tile_lin_transpose_t_kernel(tc, x, W, grad_out, out):
+    nc = tc.nc
+    with ExitStack() as ctx:
+        ctx.enter_context(tc.manual_schedule())
+        const = ctx.enter_context(tc.tile_pool(name="const", bufs=1))
+        raw = ctx.enter_context(tc.tile_pool(name="raw", bufs=1))
+        grp = ctx.enter_context(tc.tile_pool(name="grp", bufs=3))
+        cod = ctx.enter_context(tc.tile_pool(name="cod", bufs=3))
+        epi = ctx.enter_context(tc.tile_pool(name="epi", bufs=1))
+        psum = ctx.enter_context(tc.psum_pool(name="psum", bufs=1))
+
+        ident = const.tile([P, P], F32, name="ident")
+        make_identity(nc, ident[:])
+        anti = const.tile([P, P], F32, name="anti")
+        nc.gpsimd.memset(anti[:], 0.0)
+        nc.gpsimd.affine_select(
+            out=anti[:],
+            in_=anti[:],
+            compare_op=ALU.not_equal,
+            fill=1.0,
+            base=-(P - 1),
+            pattern=[[1, P]],
+            channel_multiplier=1,
+        )
+
+        xr = []
+        gr = []
+        for c in range(PASSES):
+            rows = slice(c * K_PASS, (c + 1) * K_PASS)
+            xt = raw.tile([P, PACK, WIDTH], BF16, name="xr%d" % c)
+            nc.sync.dma_start(out=xt[:], in_=x[rows, :].rearrange("(p t) w -> p t w", t=PACK))
+            gt = raw.tile([P, PACK, WIDTH], BF16, name="gr%d" % c)
+            nc.sync.dma_start(out=gt[:], in_=grad_out[rows, :].rearrange("(p t) w -> p t w", t=PACK))
+            xr.append(xt)
+            gr.append(gt)
+
+        m_ps = [psum.tile([P, WIDTH], F32, name="m%d" % a, tag="m%d" % a) for a in range(NT)]
+
+        for c in range(PASSES):
+            xg = grp.tile([P, WIDTH, PACK], BF16, name="xg", align_bytes=64)
+            nc.scalar.copy(
+                out=xg[:].rearrange("p (c i) t -> p c t i", i=4),
+                in_=xr[c][:].rearrange("p t (c i) -> p c t i", i=4),
+            )
+            gg = grp.tile([P, WIDTH, PACK], BF16, name="gg", align_bytes=64)
+            nc.vector.tensor_copy(
+                out=gg[:].rearrange("p (c i) t -> p c t i", i=4),
+                in_=gr[c][:].rearrange("p t (c i) -> p c t i", i=4),
+            )
+            xc = cod.tile([P, WIDTH], U32, name="xc", align_bytes=64)
+            xs = cod.tile([P, WIDTH], U8, name="xs", align_bytes=64)
+            nc.vector.quantize_mx(
+                out=xc[:].bitcast(E4), scales=xs[:], in_=xg[:].rearrange("p w t -> p (w t)")
+            )
+            gc = cod.tile([P, WIDTH], U32, name="gc", align_bytes=64)
+            gs = cod.tile([P, WIDTH], U8, name="gs", align_bytes=64)
+            nc.vector.quantize_mx(
+                out=gc[:].bitcast(E5), scales=gs[:], in_=gg[:].rearrange("p w t -> p (w t)")
+            )
+            for a in range(NT):
+                cols = slice(a * P, (a + 1) * P)
+                nc.tensor.matmul_mx(
+                    out=m_ps[a][:],
+                    lhsT=xc[:, cols].bitcast(E4),
+                    lhsT_scale=xs[:, cols],
+                    rhs=gc[:].bitcast(E5),
+                    rhs_scale=gs[:],
+                    start=(c == 0),
+                    stop=(c == PASSES - 1),
+                )
+
+        m_sb = [epi.tile([P, WIDTH + 4], F32, name="msb%d" % b) for b in range(NT)]
+        for b in range(NT):
+            if b % 2 == 0:
+                nc.scalar.copy(out=m_sb[b][:, 0:WIDTH], in_=m_ps[b][:])
+                nc.scalar.copy(out=m_sb[b][:, WIDTH : WIDTH + 1], in_=m_ps[b][:, 0:1])
+            else:
+                nc.vector.tensor_copy(out=m_sb[b][:, 0:WIDTH], in_=m_ps[b][:])
+                nc.vector.tensor_copy(out=m_sb[b][:, WIDTH : WIDTH + 1], in_=m_ps[b][:, 0:1])
+
+        t_ps = [psum.tile([P, WIDTH], F32, name="t%d" % a, tag="t%d" % a) for a in range(NT)]
+        for b in range(NT):
+            for a in range(NT):
+                nc.tensor.transpose(
+                    t_ps[a][:, b * P : (b + 1) * P], m_sb[b][:, a * P : (a + 1) * P], ident[:]
+                )
+
+        t2_sb = [epi.tile([P, WIDTH + 4], F32, name="t2sb%d" % b) for b in range(NT)]
+        s2_sb = [epi.tile([P, WIDTH], F32, name="s2sb%d" % b) for b in range(NT)]
+        dirs = [epi.tile([P, WIDTH], F32, name="dir%d" % b) for b in range(NT)]
+        for a in range(NT):
+            nc.scalar.mul(out=t2_sb[a][:, 0:WIDTH], in_=t_ps[a][:], mul=2.0)
+            nc.scalar.mul(out=t2_sb[a][:, WIDTH : WIDTH + 1], in_=t_ps[a][:, 0:1], mul=2.0)
+            nc.vector.scalar_tensor_tensor(
+                out=s2_sb[a][:],
+                in0=m_sb[a][:, 0:WIDTH],
+                scalar=2.0,
+                in1=t2_sb[a][:, 0:WIDTH],
+                op0=ALU.mult,
+                op1=ALU.add,
+            )
+            nc.gpsimd.tensor_tensor(
+                out=dirs[a][:], in0=t2_sb[a][:, 0:WIDTH], in1=m_sb[a][:, 1 : WIDTH + 1], op=ALU.add
+            )
+
+        f_ps = [psum.tile([P, WIDTH], F32, name="f%d" % a, tag="m%d" % a) for a in range(NT)]
+        done = [0] * NT
+        per_bank = 4 * NT
+
+        def add_t(a, blk, src, perm):
+            nc.tensor.matmul(
+                out=f_ps[a][:, blk * P : (blk + 1) * P],
+                lhsT=src,
+                rhs=perm[:],
+                is_transpose=True,
+                start=(done[a] == 0),
+                stop=(done[a] == per_bank - 1),
+            )
+            done[a] += 1
+
+        r2_sb = [epi.tile([P, WIDTH], F32, name="r2sb%d" % b) for b in range(NT)]
+        for b in range(NT):
+            if b < 2:
+                nc.scalar.copy(out=r2_sb[b][:], in_=s2_sb[b][:, ::-1])
+            else:
+                nc.vector.tensor_copy(out=r2_sb[b][:], in_=s2_sb[b][:, ::-1])
+
+        for b in range(NT):
+            for a in range(NT):
+                add_t(a, b, t2_sb[b][:, a * P + 1 : (a + 1) * P + 1], ident)
+            for a in range(NT):
+                add_t(a, NT - 1 - b, s2_sb[b][:, a * P : (a + 1) * P], anti)
+        for a in range(NT):
+            for b in range(NT):
+                add_t(a, b, r2_sb[b][:, a * P : (a + 1) * P], ident)
+                add_t(a, NT - 1 - b, r2_sb[b][:, a * P : (a + 1) * P], anti)
+
+        for a in range(NT):
+            o_sb = epi.tile([P, WIDTH], F32, name="o%d" % a)
+            nc.vector.scalar_tensor_tensor(
+                out=o_sb[:], in0=f_ps[a][:], scalar=0.5, in1=dirs[a][:], op0=ALU.mult, op1=ALU.add
+            )
+            nc.sync.dma_start(out=out[a * P : (a + 1) * P, :], in_=o_sb[:])

@@ -20,6 +20,7 @@ TOKENS = 8192
 WIDTH = 512
 PASSES = TOKENS // K_PASS
 NT = WIDTH // P
+G_SPLIT = 164
 
 FLOPS = 2 * TOKENS * WIDTH * WIDTH
 BYTES = 2 * TOKENS * WIDTH * 2 + WIDTH * WIDTH * 4
@@ -55,15 +56,27 @@ def tile_lin_transpose_t_kernel(tc, x, W, grad_out, out):
         for c in range(PASSES):
             rows = slice(c * K_PASS, (c + 1) * K_PASS)
             xt = raw.tile([P, PACK, WIDTH], BF16, name="xr%d" % c)
-            nc.sync.dma_start(out=xt[:], in_=x[rows, :].rearrange("(p t) w -> p t w", t=PACK))
             gt = raw.tile([P, PACK, WIDTH], BF16, name="gr%d" % c)
-            nc.sync.dma_start(out=gt[:], in_=grad_out[rows, :].rearrange("(p t) w -> p t w", t=PACK))
+            x_src = x[rows, :].rearrange("(p t) w -> p t w", t=PACK)
+            g_src = grad_out[rows, :].rearrange("(p t) w -> p t w", t=PACK)
+            if c < PASSES - 1:
+                nc.sync.dma_start(out=xt[:], in_=x_src)
+                nc.sync.dma_start(out=gt[:], in_=g_src)
+            else:
+                nc.sync.dma_start(out=gt[:], in_=g_src)
+                nc.sync.dma_start(out=xt[:], in_=x_src)
             xr.append(xt)
             gr.append(gt)
 
+        def regroup(copy, dst, src, w0, w1):
+            copy(
+                out=dst[:, w0:w1, :].rearrange("p (c i) t -> p c t i", i=4),
+                in_=src[:, :, w0:w1].rearrange("p t (c i) -> p c t i", i=4),
+            )
+
         m_ps = [psum.tile([P, WIDTH], F32, name="m%d" % a, tag="m%d" % a) for a in range(NT)]
 
-        for c in range(PASSES):
+        for c in range(PASSES - 1):
             xg = grp.tile([P, WIDTH, PACK], BF16, name="xg", align_bytes=64)
             nc.scalar.copy(
                 out=xg[:].rearrange("p (c i) t -> p c t i", i=4),
@@ -95,6 +108,45 @@ def tile_lin_transpose_t_kernel(tc, x, W, grad_out, out):
                     start=(c == 0),
                     stop=(c == PASSES - 1),
                 )
+
+        c = PASSES - 1
+        gg = grp.tile([P, WIDTH, PACK], BF16, name="gg", align_bytes=64)
+        xg = grp.tile([P, WIDTH, PACK], BF16, name="xg", align_bytes=64)
+        xc = cod.tile([P, WIDTH], U32, name="xc", align_bytes=64)
+        xs = cod.tile([P, WIDTH], U8, name="xs", align_bytes=64)
+        gc = cod.tile([P, WIDTH], U32, name="gc", align_bytes=64)
+        gs = cod.tile([P, WIDTH], U8, name="gs", align_bytes=64)
+        regroup(nc.scalar.copy, gg, gr[c], G_SPLIT, WIDTH)
+        regroup(nc.vector.tensor_copy, gg, gr[c], 0, G_SPLIT)
+        regroup(nc.scalar.copy, xg, xr[c], 0, P)
+        regroup(nc.scalar.copy, xg, xr[c], P, 2 * P)
+        nc.vector.quantize_mx(
+            out=gc[:].bitcast(E5), scales=gs[:], in_=gg[:].rearrange("p w t -> p (w t)")
+        )
+
+        def last_quant(a):
+            cols = slice(a * P, (a + 1) * P)
+            nc.vector.quantize_mx(
+                out=xc[:, cols].bitcast(E4),
+                scales=xs[:, cols],
+                in_=xg[:, cols, :].rearrange("p w t -> p (w t)"),
+            )
+            nc.tensor.matmul_mx(
+                out=m_ps[a][:],
+                lhsT=xc[:, cols].bitcast(E4),
+                lhsT_scale=xs[:, cols],
+                rhs=gc[:].bitcast(E5),
+                rhs_scale=gs[:],
+                start=False,
+                stop=True,
+            )
+
+        last_quant(0)
+        regroup(nc.vector.tensor_copy, xg, xr[c], 2 * P, 3 * P)
+        last_quant(1)
+        regroup(nc.vector.tensor_copy, xg, xr[c], 3 * P, 4 * P)
+        last_quant(2)
+        last_quant(3)
 
         m_sb = [epi.tile([P, WIDTH + 4], F32, name="msb%d" % b) for b in range(NT)]
         for b in range(NT):
@@ -164,7 +216,16 @@ def tile_lin_transpose_t_kernel(tc, x, W, grad_out, out):
 
         for a in range(NT):
             o_sb = epi.tile([P, WIDTH], F32, name="o%d" % a)
-            nc.vector.scalar_tensor_tensor(
-                out=o_sb[:], in0=f_ps[a][:], scalar=0.5, in1=dirs[a][:], op0=ALU.mult, op1=ALU.add
-            )
-            nc.sync.dma_start(out=out[a * P : (a + 1) * P, :], in_=o_sb[:])
+            pieces = 2 if a == NT - 1 else 1
+            step = WIDTH // pieces
+            for h in range(pieces):
+                cols = slice(h * step, (h + 1) * step)
+                nc.vector.scalar_tensor_tensor(
+                    out=o_sb[:, cols],
+                    in0=f_ps[a][:, cols],
+                    scalar=0.5,
+                    in1=dirs[a][:, cols],
+                    op0=ALU.mult,
+                    op1=ALU.add,
+                )
+                nc.sync.dma_start(out=out[a * P : (a + 1) * P, cols], in_=o_sb[:, cols])

@@ -20,7 +20,6 @@ TOKENS = 8192
 WIDTH = 512
 PASSES = TOKENS // K_PASS
 NT = WIDTH // P
-G_SPLIT = 164
 
 FLOPS = 2 * TOKENS * WIDTH * WIDTH
 BYTES = 2 * TOKENS * WIDTH * 2 + WIDTH * WIDTH * 4
@@ -59,9 +58,12 @@ def tile_lin_transpose_t_kernel(tc, x, W, grad_out, out):
             gt = raw.tile([P, PACK, WIDTH], BF16, name="gr%d" % c)
             x_src = x[rows, :].rearrange("(p t) w -> p t w", t=PACK)
             g_src = grad_out[rows, :].rearrange("(p t) w -> p t w", t=PACK)
-            if c < PASSES - 1:
-                nc.sync.dma_start(out=xt[:], in_=x_src)
-                nc.sync.dma_start(out=gt[:], in_=g_src)
+            if c == 0:
+                half = WIDTH // 2
+                for h in range(2):
+                    cols = slice(h * half, (h + 1) * half)
+                    nc.sync.dma_start(out=gt[:, :, cols], in_=g_src[:, :, cols])
+                    nc.sync.dma_start(out=xt[:, :, cols], in_=x_src[:, :, cols])
             else:
                 nc.sync.dma_start(out=gt[:], in_=g_src)
                 nc.sync.dma_start(out=xt[:], in_=x_src)
@@ -76,75 +78,67 @@ def tile_lin_transpose_t_kernel(tc, x, W, grad_out, out):
 
         m_ps = [psum.tile([P, WIDTH], F32, name="m%d" % a, tag="m%d" % a) for a in range(NT)]
 
-        for c in range(PASSES - 1):
-            xg = grp.tile([P, WIDTH, PACK], BF16, name="xg", align_bytes=64)
-            nc.scalar.copy(
-                out=xg[:].rearrange("p (c i) t -> p c t i", i=4),
-                in_=xr[c][:].rearrange("p t (c i) -> p c t i", i=4),
-            )
-            gg = grp.tile([P, WIDTH, PACK], BF16, name="gg", align_bytes=64)
-            nc.vector.tensor_copy(
-                out=gg[:].rearrange("p (c i) t -> p c t i", i=4),
-                in_=gr[c][:].rearrange("p t (c i) -> p c t i", i=4),
-            )
-            xc = cod.tile([P, WIDTH], U32, name="xc", align_bytes=64)
-            xs = cod.tile([P, WIDTH], U8, name="xs", align_bytes=64)
+        def quant(dst, planes, src, fmt):
             nc.vector.quantize_mx(
-                out=xc[:].bitcast(E4), scales=xs[:], in_=xg[:].rearrange("p w t -> p (w t)")
+                out=dst.bitcast(fmt), scales=planes, in_=src.rearrange("p w t -> p (w t)")
             )
-            gc = cod.tile([P, WIDTH], U32, name="gc", align_bytes=64)
-            gs = cod.tile([P, WIDTH], U8, name="gs", align_bytes=64)
-            nc.vector.quantize_mx(
-                out=gc[:].bitcast(E5), scales=gs[:], in_=gg[:].rearrange("p w t -> p (w t)")
-            )
-            for a in range(NT):
-                cols = slice(a * P, (a + 1) * P)
-                nc.tensor.matmul_mx(
-                    out=m_ps[a][:],
-                    lhsT=xc[:, cols].bitcast(E4),
-                    lhsT_scale=xs[:, cols],
-                    rhs=gc[:].bitcast(E5),
-                    rhs_scale=gs[:],
-                    start=(c == 0),
-                    stop=(c == PASSES - 1),
-                )
 
-        c = PASSES - 1
-        gg = grp.tile([P, WIDTH, PACK], BF16, name="gg", align_bytes=64)
-        xg = grp.tile([P, WIDTH, PACK], BF16, name="xg", align_bytes=64)
-        xc = cod.tile([P, WIDTH], U32, name="xc", align_bytes=64)
-        xs = cod.tile([P, WIDTH], U8, name="xs", align_bytes=64)
-        gc = cod.tile([P, WIDTH], U32, name="gc", align_bytes=64)
-        gs = cod.tile([P, WIDTH], U8, name="gs", align_bytes=64)
-        regroup(nc.scalar.copy, gg, gr[c], G_SPLIT, WIDTH)
-        regroup(nc.vector.tensor_copy, gg, gr[c], 0, G_SPLIT)
-        regroup(nc.scalar.copy, xg, xr[c], 0, P)
-        regroup(nc.scalar.copy, xg, xr[c], P, 2 * P)
-        nc.vector.quantize_mx(
-            out=gc[:].bitcast(E5), scales=gs[:], in_=gg[:].rearrange("p w t -> p (w t)")
-        )
-
-        def last_quant(a):
+        def mx_pass(a, xc, xs, gc, gs, first, last):
             cols = slice(a * P, (a + 1) * P)
-            nc.vector.quantize_mx(
-                out=xc[:, cols].bitcast(E4),
-                scales=xs[:, cols],
-                in_=xg[:, cols, :].rearrange("p w t -> p (w t)"),
-            )
             nc.tensor.matmul_mx(
                 out=m_ps[a][:],
                 lhsT=xc[:, cols].bitcast(E4),
                 lhsT_scale=xs[:, cols],
                 rhs=gc[:].bitcast(E5),
                 rhs_scale=gs[:],
-                start=False,
-                stop=True,
+                start=first,
+                stop=last,
             )
 
+        xgs = []
+        g_codes = []
+        for c in range(PASSES):
+            gg = grp.tile([P, WIDTH, PACK], BF16, name="gg", align_bytes=64)
+            if c == 0:
+                regroup(nc.vector.tensor_copy, gg, gr[c], 0, WIDTH // 2)
+                regroup(nc.vector.tensor_copy, gg, gr[c], WIDTH // 2, WIDTH)
+            else:
+                regroup(nc.vector.tensor_copy, gg, gr[c], 0, WIDTH)
+            if c > 0:
+                xc = cod.tile([P, WIDTH], U32, name="xc", align_bytes=64)
+                xs = cod.tile([P, WIDTH], U8, name="xs", align_bytes=64)
+                quant(xc[:], xs[:], xgs[c - 1][:], E4)
+            gc = cod.tile([P, WIDTH], U32, name="gc", align_bytes=64)
+            gs = cod.tile([P, WIDTH], U8, name="gs", align_bytes=64)
+            quant(gc[:], gs[:], gg[:], E5)
+            g_codes.append((gc, gs))
+            if c > 0:
+                for a in range(NT):
+                    mx_pass(a, xc, xs, g_codes[c - 1][0], g_codes[c - 1][1], c == 1, False)
+            xg = grp.tile([P, WIDTH, PACK], BF16, name="xg", align_bytes=64)
+            xgs.append(xg)
+            if c == 0:
+                regroup(nc.scalar.copy, xg, xr[c], 0, WIDTH // 2)
+                regroup(nc.scalar.copy, xg, xr[c], WIDTH // 2, WIDTH)
+            elif c < PASSES - 1:
+                regroup(nc.scalar.copy, xg, xr[c], 0, WIDTH)
+
+        c = PASSES - 1
+        xg = xgs[c]
+        gc, gs = g_codes[c]
+        xc = cod.tile([P, WIDTH], U32, name="xc", align_bytes=64)
+        xs = cod.tile([P, WIDTH], U8, name="xs", align_bytes=64)
+        for a in range(NT - 1):
+            regroup(nc.scalar.copy, xg, xr[c], a * P, (a + 1) * P)
+
+        def last_quant(a):
+            cols = slice(a * P, (a + 1) * P)
+            quant(xc[:, cols], xs[:, cols], xg[:, cols, :], E4)
+            mx_pass(a, xc, xs, gc, gs, False, True)
+
         last_quant(0)
-        regroup(nc.vector.tensor_copy, xg, xr[c], 2 * P, 3 * P)
+        regroup(nc.vector.tensor_copy, xg, xr[c], (NT - 1) * P, NT * P)
         last_quant(1)
-        regroup(nc.vector.tensor_copy, xg, xr[c], 3 * P, 4 * P)
         last_quant(2)
         last_quant(3)
 

@@ -20,6 +20,7 @@ TOKENS = 8192
 WIDTH = 512
 PASSES = TOKENS // K_PASS
 NT = WIDTH // P
+G_SPLIT = 164
 
 FLOPS = 2 * TOKENS * WIDTH * WIDTH
 BYTES = 2 * TOKENS * WIDTH * 2 + WIDTH * WIDTH * 4
@@ -58,12 +59,9 @@ def tile_lin_transpose_t_kernel(tc, x, W, grad_out, out):
             gt = raw.tile([P, PACK, WIDTH], BF16, name="gr%d" % c)
             x_src = x[rows, :].rearrange("(p t) w -> p t w", t=PACK)
             g_src = grad_out[rows, :].rearrange("(p t) w -> p t w", t=PACK)
-            if c == 0:
-                half = WIDTH // 2
-                for h in range(2):
-                    cols = slice(h * half, (h + 1) * half)
-                    nc.sync.dma_start(out=gt[:, :, cols], in_=g_src[:, :, cols])
-                    nc.sync.dma_start(out=xt[:, :, cols], in_=x_src[:, :, cols])
+            if c < PASSES - 1:
+                nc.sync.dma_start(out=xt[:], in_=x_src)
+                nc.sync.dma_start(out=gt[:], in_=g_src)
             else:
                 nc.sync.dma_start(out=gt[:], in_=g_src)
                 nc.sync.dma_start(out=xt[:], in_=x_src)
@@ -78,67 +76,75 @@ def tile_lin_transpose_t_kernel(tc, x, W, grad_out, out):
 
         m_ps = [psum.tile([P, WIDTH], F32, name="m%d" % a, tag="m%d" % a) for a in range(NT)]
 
-        def quant(dst, planes, src, fmt):
-            nc.vector.quantize_mx(
-                out=dst.bitcast(fmt), scales=planes, in_=src.rearrange("p w t -> p (w t)")
+        for c in range(PASSES - 1):
+            xg = grp.tile([P, WIDTH, PACK], BF16, name="xg", align_bytes=64)
+            nc.scalar.copy(
+                out=xg[:].rearrange("p (c i) t -> p c t i", i=4),
+                in_=xr[c][:].rearrange("p t (c i) -> p c t i", i=4),
             )
+            gg = grp.tile([P, WIDTH, PACK], BF16, name="gg", align_bytes=64)
+            nc.vector.tensor_copy(
+                out=gg[:].rearrange("p (c i) t -> p c t i", i=4),
+                in_=gr[c][:].rearrange("p t (c i) -> p c t i", i=4),
+            )
+            xc = cod.tile([P, WIDTH], U32, name="xc", align_bytes=64)
+            xs = cod.tile([P, WIDTH], U8, name="xs", align_bytes=64)
+            nc.vector.quantize_mx(
+                out=xc[:].bitcast(E4), scales=xs[:], in_=xg[:].rearrange("p w t -> p (w t)")
+            )
+            gc = cod.tile([P, WIDTH], U32, name="gc", align_bytes=64)
+            gs = cod.tile([P, WIDTH], U8, name="gs", align_bytes=64)
+            nc.vector.quantize_mx(
+                out=gc[:].bitcast(E5), scales=gs[:], in_=gg[:].rearrange("p w t -> p (w t)")
+            )
+            for a in range(NT):
+                cols = slice(a * P, (a + 1) * P)
+                nc.tensor.matmul_mx(
+                    out=m_ps[a][:],
+                    lhsT=xc[:, cols].bitcast(E4),
+                    lhsT_scale=xs[:, cols],
+                    rhs=gc[:].bitcast(E5),
+                    rhs_scale=gs[:],
+                    start=(c == 0),
+                    stop=(c == PASSES - 1),
+                )
 
-        def mx_pass(a, xc, xs, gc, gs, first, last):
+        c = PASSES - 1
+        gg = grp.tile([P, WIDTH, PACK], BF16, name="gg", align_bytes=64)
+        xg = grp.tile([P, WIDTH, PACK], BF16, name="xg", align_bytes=64)
+        xc = cod.tile([P, WIDTH], U32, name="xc", align_bytes=64)
+        xs = cod.tile([P, WIDTH], U8, name="xs", align_bytes=64)
+        gc = cod.tile([P, WIDTH], U32, name="gc", align_bytes=64)
+        gs = cod.tile([P, WIDTH], U8, name="gs", align_bytes=64)
+        regroup(nc.scalar.copy, gg, gr[c], G_SPLIT, WIDTH)
+        regroup(nc.vector.tensor_copy, gg, gr[c], 0, G_SPLIT)
+        regroup(nc.scalar.copy, xg, xr[c], 0, P)
+        regroup(nc.scalar.copy, xg, xr[c], P, 2 * P)
+        nc.vector.quantize_mx(
+            out=gc[:].bitcast(E5), scales=gs[:], in_=gg[:].rearrange("p w t -> p (w t)")
+        )
+
+        def last_quant(a):
             cols = slice(a * P, (a + 1) * P)
+            nc.vector.quantize_mx(
+                out=xc[:, cols].bitcast(E4),
+                scales=xs[:, cols],
+                in_=xg[:, cols, :].rearrange("p w t -> p (w t)"),
+            )
             nc.tensor.matmul_mx(
                 out=m_ps[a][:],
                 lhsT=xc[:, cols].bitcast(E4),
                 lhsT_scale=xs[:, cols],
                 rhs=gc[:].bitcast(E5),
                 rhs_scale=gs[:],
-                start=first,
-                stop=last,
+                start=False,
+                stop=True,
             )
 
-        xgs = []
-        g_codes = []
-        for c in range(PASSES):
-            gg = grp.tile([P, WIDTH, PACK], BF16, name="gg", align_bytes=64)
-            if c == 0:
-                regroup(nc.vector.tensor_copy, gg, gr[c], 0, WIDTH // 2)
-                regroup(nc.vector.tensor_copy, gg, gr[c], WIDTH // 2, WIDTH)
-            else:
-                regroup(nc.vector.tensor_copy, gg, gr[c], 0, WIDTH)
-            if c > 0:
-                xc = cod.tile([P, WIDTH], U32, name="xc", align_bytes=64)
-                xs = cod.tile([P, WIDTH], U8, name="xs", align_bytes=64)
-                quant(xc[:], xs[:], xgs[c - 1][:], E4)
-            gc = cod.tile([P, WIDTH], U32, name="gc", align_bytes=64)
-            gs = cod.tile([P, WIDTH], U8, name="gs", align_bytes=64)
-            quant(gc[:], gs[:], gg[:], E5)
-            g_codes.append((gc, gs))
-            if c > 0:
-                for a in range(NT):
-                    mx_pass(a, xc, xs, g_codes[c - 1][0], g_codes[c - 1][1], c == 1, False)
-            xg = grp.tile([P, WIDTH, PACK], BF16, name="xg", align_bytes=64)
-            xgs.append(xg)
-            if c == 0:
-                regroup(nc.scalar.copy, xg, xr[c], 0, WIDTH // 2)
-                regroup(nc.scalar.copy, xg, xr[c], WIDTH // 2, WIDTH)
-            elif c < PASSES - 1:
-                regroup(nc.scalar.copy, xg, xr[c], 0, WIDTH)
-
-        c = PASSES - 1
-        xg = xgs[c]
-        gc, gs = g_codes[c]
-        xc = cod.tile([P, WIDTH], U32, name="xc", align_bytes=64)
-        xs = cod.tile([P, WIDTH], U8, name="xs", align_bytes=64)
-        for a in range(NT - 1):
-            regroup(nc.scalar.copy, xg, xr[c], a * P, (a + 1) * P)
-
-        def last_quant(a):
-            cols = slice(a * P, (a + 1) * P)
-            quant(xc[:, cols], xs[:, cols], xg[:, cols, :], E4)
-            mx_pass(a, xc, xs, gc, gs, False, True)
-
         last_quant(0)
-        regroup(nc.vector.tensor_copy, xg, xr[c], (NT - 1) * P, NT * P)
+        regroup(nc.vector.tensor_copy, xg, xr[c], 2 * P, 3 * P)
         last_quant(1)
+        regroup(nc.vector.tensor_copy, xg, xr[c], 3 * P, 4 * P)
         last_quant(2)
         last_quant(3)
 
@@ -158,22 +164,23 @@ def tile_lin_transpose_t_kernel(tc, x, W, grad_out, out):
                     t_ps[a][:, b * P : (b + 1) * P], m_sb[b][:, a * P : (a + 1) * P], ident[:]
                 )
 
-        t2_sb = [epi.tile([P, WIDTH + 4], F32, name="t2sb%d" % b) for b in range(NT)]
-        s2_sb = [epi.tile([P, WIDTH], F32, name="s2sb%d" % b) for b in range(NT)]
+        t_sb = [epi.tile([P, WIDTH + 4], F32, name="tsb%d" % b) for b in range(NT)]
+        s_sb = [epi.tile([P, WIDTH], F32, name="ssb%d" % b) for b in range(NT)]
         dirs = [epi.tile([P, WIDTH], F32, name="dir%d" % b) for b in range(NT)]
         for a in range(NT):
-            nc.scalar.mul(out=t2_sb[a][:, 0:WIDTH], in_=t_ps[a][:], mul=2.0)
-            nc.scalar.mul(out=t2_sb[a][:, WIDTH : WIDTH + 1], in_=t_ps[a][:, 0:1], mul=2.0)
+            nc.scalar.copy(out=t_sb[a][:, 0:WIDTH], in_=t_ps[a][:])
+            nc.scalar.copy(out=t_sb[a][:, WIDTH : WIDTH + 1], in_=t_ps[a][:, 0:1])
+            nc.vector.tensor_tensor(
+                out=s_sb[a][:], in0=m_sb[a][:, 0:WIDTH], in1=t_sb[a][:, 0:WIDTH], op=ALU.add
+            )
+        for a in range(NT):
             nc.vector.scalar_tensor_tensor(
-                out=s2_sb[a][:],
-                in0=m_sb[a][:, 0:WIDTH],
+                out=dirs[a][:],
+                in0=t_sb[a][:, 0:WIDTH],
                 scalar=2.0,
-                in1=t2_sb[a][:, 0:WIDTH],
+                in1=m_sb[a][:, 1 : WIDTH + 1],
                 op0=ALU.mult,
                 op1=ALU.add,
-            )
-            nc.gpsimd.tensor_tensor(
-                out=dirs[a][:], in0=t2_sb[a][:, 0:WIDTH], in1=m_sb[a][:, 1 : WIDTH + 1], op=ALU.add
             )
 
         f_ps = [psum.tile([P, WIDTH], F32, name="f%d" % a, tag="m%d" % a) for a in range(NT)]
@@ -191,22 +198,19 @@ def tile_lin_transpose_t_kernel(tc, x, W, grad_out, out):
             )
             done[a] += 1
 
-        r2_sb = [epi.tile([P, WIDTH], F32, name="r2sb%d" % b) for b in range(NT)]
+        r_sb = [epi.tile([P, WIDTH], F32, name="rsb%d" % b) for b in range(NT)]
         for b in range(NT):
-            if b < 2:
-                nc.scalar.copy(out=r2_sb[b][:], in_=s2_sb[b][:, ::-1])
-            else:
-                nc.vector.tensor_copy(out=r2_sb[b][:], in_=s2_sb[b][:, ::-1])
+            nc.scalar.copy(out=r_sb[b][:], in_=s_sb[b][:, ::-1])
 
         for b in range(NT):
             for a in range(NT):
-                add_t(a, b, t2_sb[b][:, a * P + 1 : (a + 1) * P + 1], ident)
+                add_t(a, b, t_sb[b][:, a * P + 1 : (a + 1) * P + 1], ident)
             for a in range(NT):
-                add_t(a, NT - 1 - b, s2_sb[b][:, a * P : (a + 1) * P], anti)
+                add_t(a, NT - 1 - b, s_sb[b][:, a * P : (a + 1) * P], anti)
         for a in range(NT):
             for b in range(NT):
-                add_t(a, b, r2_sb[b][:, a * P : (a + 1) * P], ident)
-                add_t(a, NT - 1 - b, r2_sb[b][:, a * P : (a + 1) * P], anti)
+                add_t(a, b, r_sb[b][:, a * P : (a + 1) * P], ident)
+                add_t(a, NT - 1 - b, r_sb[b][:, a * P : (a + 1) * P], anti)
 
         for a in range(NT):
             o_sb = epi.tile([P, WIDTH], F32, name="o%d" % a)
@@ -214,12 +218,7 @@ def tile_lin_transpose_t_kernel(tc, x, W, grad_out, out):
             step = WIDTH // pieces
             for h in range(pieces):
                 cols = slice(h * step, (h + 1) * step)
-                nc.vector.scalar_tensor_tensor(
-                    out=o_sb[:, cols],
-                    in0=f_ps[a][:, cols],
-                    scalar=0.5,
-                    in1=dirs[a][:, cols],
-                    op0=ALU.mult,
-                    op1=ALU.add,
+                nc.vector.tensor_tensor(
+                    out=o_sb[:, cols], in0=f_ps[a][:, cols], in1=dirs[a][:, cols], op=ALU.add
                 )
                 nc.sync.dma_start(out=out[a * P : (a + 1) * P, cols], in_=o_sb[:, cols])

@@ -150,12 +150,12 @@ def tile_lin_transpose_t_kernel(tc, x, W, grad_out, out):
 
         m_sb = [epi.tile([P, WIDTH + 4], F32, name="msb%d" % b) for b in range(NT)]
         for b in range(NT):
-            if b % 2 == 0:
+            if b < NT - 1:
                 nc.scalar.copy(out=m_sb[b][:, 0:WIDTH], in_=m_ps[b][:])
-                nc.scalar.copy(out=m_sb[b][:, WIDTH : WIDTH + 1], in_=m_ps[b][:, 0:1])
             else:
                 nc.vector.tensor_copy(out=m_sb[b][:, 0:WIDTH], in_=m_ps[b][:])
-                nc.vector.tensor_copy(out=m_sb[b][:, WIDTH : WIDTH + 1], in_=m_ps[b][:, 0:1])
+        for b in range(NT):
+            nc.scalar.copy(out=m_sb[b][:, WIDTH : WIDTH + 1], in_=m_sb[b][:, 0:1])
 
         t_ps = [psum.tile([P, WIDTH], F32, name="t%d" % a, tag="t%d" % a) for a in range(NT)]
         for b in range(NT):
@@ -169,10 +169,11 @@ def tile_lin_transpose_t_kernel(tc, x, W, grad_out, out):
         dirs = [epi.tile([P, WIDTH], F32, name="dir%d" % b) for b in range(NT)]
         for a in range(NT):
             nc.scalar.copy(out=t_sb[a][:, 0:WIDTH], in_=t_ps[a][:])
-            nc.scalar.copy(out=t_sb[a][:, WIDTH : WIDTH + 1], in_=t_ps[a][:, 0:1])
             nc.vector.tensor_tensor(
                 out=s_sb[a][:], in0=m_sb[a][:, 0:WIDTH], in1=t_sb[a][:, 0:WIDTH], op=ALU.add
             )
+        for a in range(NT):
+            nc.scalar.copy(out=t_sb[a][:, WIDTH : WIDTH + 1], in_=t_sb[a][:, 0:1])
         for a in range(NT):
             nc.vector.scalar_tensor_tensor(
                 out=dirs[a][:],
@@ -203,10 +204,13 @@ def tile_lin_transpose_t_kernel(tc, x, W, grad_out, out):
             nc.scalar.copy(out=r_sb[b][:], in_=s_sb[b][:, ::-1])
 
         for b in range(NT):
-            for a in range(NT):
+            for a in range(NT - 1):
                 add_t(a, b, t_sb[b][:, a * P + 1 : (a + 1) * P + 1], ident)
             for a in range(NT):
                 add_t(a, NT - 1 - b, s_sb[b][:, a * P : (a + 1) * P], anti)
+        for b in range(NT):
+            a = NT - 1
+            add_t(a, b, t_sb[b][:, a * P + 1 : (a + 1) * P + 1], ident)
         for a in range(NT):
             for b in range(NT):
                 add_t(a, b, r_sb[b][:, a * P : (a + 1) * P], ident)

@@ -21,6 +21,7 @@ WIDTH = 512
 PASSES = TOKENS // K_PASS
 NT = WIDTH // P
 G_SPLIT = 164
+RUN = 8
 
 FLOPS = 2 * TOKENS * WIDTH * WIDTH
 BYTES = 2 * TOKENS * WIDTH * 2 + WIDTH * WIDTH * 4
@@ -79,13 +80,13 @@ def tile_lin_transpose_t_kernel(tc, x, W, grad_out, out):
         for c in range(PASSES - 1):
             xg = grp.tile([P, WIDTH, PACK], BF16, name="xg", align_bytes=64)
             nc.scalar.copy(
-                out=xg[:].rearrange("p (c i) t -> p c t i", i=4),
-                in_=xr[c][:].rearrange("p t (c i) -> p c t i", i=4),
+                out=xg[:].rearrange("p (c i) t -> p c t i", i=RUN),
+                in_=xr[c][:].rearrange("p t (c i) -> p c t i", i=RUN),
             )
             gg = grp.tile([P, WIDTH, PACK], BF16, name="gg", align_bytes=64)
             nc.vector.tensor_copy(
-                out=gg[:].rearrange("p (c i) t -> p c t i", i=4),
-                in_=gr[c][:].rearrange("p t (c i) -> p c t i", i=4),
+                out=gg[:].rearrange("p (c i) t -> p c t i", i=RUN),
+                in_=gr[c][:].rearrange("p t (c i) -> p c t i", i=RUN),
             )
             xc = cod.tile([P, WIDTH], U32, name="xc", align_bytes=64)
             xs = cod.tile([P, WIDTH], U8, name="xs", align_bytes=64)

from contextlib import ExitStack

import concourse.bass as bass
import concourse.mybir as mybir
import concourse.tile as tile
from concourse.masks import make_identity

F32 = mybir.dt.float32
BF16 = mybir.dt.bfloat16
U32 = mybir.dt.uint32
U8 = mybir.dt.uint8
E4 = mybir.dt.float8_e4m3fn_x4
E5 = mybir.dt.float8_e5m2_x4
ALU = mybir.AluOpType

P = 128
PACK = 4
K_PASS = P * PACK
TOKENS = 8192
WIDTH = 512
PASSES = TOKENS // K_PASS
NT = WIDTH // P
G_SPLIT = 164
RUN = 8

FLOPS = 2 * TOKENS * WIDTH * WIDTH
BYTES = 2 * TOKENS * WIDTH * 2 + WIDTH * WIDTH * 4


def tile_lin_transpose_t_kernel(tc, x, W, grad_out, out):
    nc = tc.nc
    with ExitStack() as ctx:
        ctx.enter_context(tc.manual_schedule())
        const = ctx.enter_context(tc.tile_pool(name="const", bufs=1))
        raw = ctx.enter_context(tc.tile_pool(name="raw", bufs=1))
        grp = ctx.enter_context(tc.tile_pool(name="grp", bufs=3))
        cod = ctx.enter_context(tc.tile_pool(name="cod", bufs=3))
        epi = ctx.enter_context(tc.tile_pool(name="epi", bufs=1))
        psum = ctx.enter_context(tc.psum_pool(name="psum", bufs=1))

        ident = const.tile([P, P], F32, name="ident")
        make_identity(nc, ident[:])
        anti = const.tile([P, P], F32, name="anti")
        nc.gpsimd.memset(anti[:], 0.0)
        nc.gpsimd.affine_select(
            out=anti[:],
            in_=anti[:],
            compare_op=ALU.not_equal,
            fill=1.0,
            base=-(P - 1),
            pattern=[[1, P]],
            channel_multiplier=1,
        )

        xr = []
        gr = []
        for c in range(PASSES):
            rows = slice(c * K_PASS, (c + 1) * K_PASS)
            xt = raw.tile([P, PACK, WIDTH], BF16, name="xr%d" % c)
            gt = raw.tile([P, PACK, WIDTH], BF16, name="gr%d" % c)
            x_src = x[rows, :].rearrange("(p t) w -> p t w", t=PACK)
            g_src = grad_out[rows, :].rearrange("(p t) w -> p t w", t=PACK)
            if c < PASSES - 1:
                nc.sync.dma_start(out=xt[:], in_=x_src)
                nc.sync.dma_start(out=gt[:], in_=g_src)
            else:
                nc.sync.dma_start(out=gt[:], in_=g_src)
                nc.sync.dma_start(out=xt[:], in_=x_src)
            xr.append(xt)
            gr.append(gt)

        def regroup(copy, dst, src, w0, w1):
            copy(
                out=dst[:, w0:w1, :].rearrange("p (c i) t -> p c t i", i=4),
                in_=src[:, :, w0:w1].rearrange("p t (c i) -> p c t i", i=4),
            )

        m_ps = [psum.tile([P, WIDTH], F32, name="m%d" % a, tag="m%d" % a) for a in range(NT)]

        for c in range(PASSES - 1):
            xg = grp.tile([P, WIDTH, PACK], BF16, name="xg", align_bytes=64)
            nc.scalar.copy(
                out=xg[:].rearrange("p (c i) t -> p c t i", i=RUN),
                in_=xr[c][:].rearrange("p t (c i) -> p c t i", i=RUN),
            )
            gg = grp.tile([P, WIDTH, PACK], BF16, name="gg", align_bytes=64)
            nc.vector.tensor_copy(
                out=gg[:].rearrange("p (c i) t -> p c t i", i=RUN),
                in_=gr[c][:].rearrange("p t (c i) -> p c t i", i=RUN),
            )
            xc = cod.tile([P, WIDTH], U32, name="xc", align_bytes=64)
            xs = cod.tile([P, WIDTH], U8, name="xs", align_bytes=64)
            nc.vector.quantize_mx(
                out=xc[:].bitcast(E4), scales=xs[:], in_=xg[:].rearrange("p w t -> p (w t)")
            )
            gc = cod.tile([P, WIDTH], U32, name="gc", align_bytes=64)
            gs = cod.tile([P, WIDTH], U8, name="gs", align_bytes=64)
            nc.vector.quantize_mx(
                out=gc[:].bitcast(E5), scales=gs[:], in_=gg[:].rearrange("p w t -> p (w t)")
            )
            for a in range(NT):
                cols = slice(a * P, (a + 1) * P)
                nc.tensor.matmul_mx(
                    out=m_ps[a][:],
                    lhsT=xc[:, cols].bitcast(E4),
                    lhsT_scale=xs[:, cols],
                    rhs=gc[:].bitcast(E5),
                    rhs_scale=gs[:],
                    start=(c == 0),
                    stop=(c == PASSES - 1),
                )

        c = PASSES - 1
        gg = grp.tile([P, WIDTH, PACK], BF16, name="gg", align_bytes=64)
        xg = grp.tile([P, WIDTH, PACK], BF16, name="xg", align_bytes=64)
        xc = cod.tile([P, WIDTH], U32, name="xc", align_bytes=64)
        xs = cod.tile([P, WIDTH], U8, name="xs", align_bytes=64)
        gc = cod.tile([P, WIDTH], U32, name="gc", align_bytes=64)
        gs = cod.tile([P, WIDTH], U8, name="gs", align_bytes=64)
        regroup(nc.scalar.copy, gg, gr[c], G_SPLIT, WIDTH)
        regroup(nc.vector.tensor_copy, gg, gr[c], 0, G_SPLIT)
        regroup(nc.scalar.copy, xg, xr[c], 0, P)
        regroup(nc.scalar.copy, xg, xr[c], P, 2 * P)
        nc.vector.quantize_mx(
            out=gc[:].bitcast(E5), scales=gs[:], in_=gg[:].rearrange("p w t -> p (w t)")
        )

        def last_quant(a):
            cols = slice(a * P, (a + 1) * P)
            nc.vector.quantize_mx(
                out=xc[:, cols].bitcast(E4),
                scales=xs[:, cols],
                in_=xg[:, cols, :].rearrange("p w t -> p (w t)"),
            )
            nc.tensor.matmul_mx(
                out=m_ps[a][:],
                lhsT=xc[:, cols].bitcast(E4),
                lhsT_scale=xs[:, cols],
                rhs=gc[:].bitcast(E5),
                rhs_scale=gs[:],
                start=False,
                stop=True,
            )

        last_quant(0)
        regroup(nc.vector.tensor_copy, xg, xr[c], 2 * P, 3 * P)
        last_quant(1)
        regroup(nc.vector.tensor_copy, xg, xr[c], 3 * P, 4 * P)
        last_quant(2)
        last_quant(3)

        m_sb = [epi.tile([P, WIDTH + 4], F32, name="msb%d" % b) for b in range(NT)]
        for b in range(NT):
            if b < NT - 1:
                nc.scalar.copy(out=m_sb[b][:, 0:WIDTH], in_=m_ps[b][:])
            else:
                nc.vector.tensor_copy(out=m_sb[b][:, 0:WIDTH], in_=m_ps[b][:])
        for b in range(NT):
            nc.scalar.copy(out=m_sb[b][:, WIDTH : WIDTH + 1], in_=m_sb[b][:, 0:1])

        t_ps = [psum.tile([P, WIDTH], F32, name="t%d" % a, tag="t%d" % a) for a in range(NT)]
        for b in range(NT):
            for a in range(NT):
                nc.tensor.transpose(
                    t_ps[a][:, b * P : (b + 1) * P], m_sb[b][:, a * P : (a + 1) * P], ident[:]
                )

        t_sb = [epi.tile([P, WIDTH + 4], F32, name="tsb%d" % b) for b in range(NT)]
        s_sb = [epi.tile([P, WIDTH], F32, name="ssb%d" % b) for b in range(NT)]
        dirs = [epi.tile([P, WIDTH], F32, name="dir%d" % b) for b in range(NT)]
        for a in range(NT):
            nc.scalar.copy(out=t_sb[a][:, 0:WIDTH], in_=t_ps[a][:])
            nc.vector.tensor_tensor(
                out=s_sb[a][:], in0=m_sb[a][:, 0:WIDTH], in1=t_sb[a][:, 0:WIDTH], op=ALU.add
            )
        for a in range(NT):
            nc.scalar.copy(out=t_sb[a][:, WIDTH : WIDTH + 1], in_=t_sb[a][:, 0:1])
        for a in range(NT):
            nc.vector.scalar_tensor_tensor(
                out=dirs[a][:],
                in0=t_sb[a][:, 0:WIDTH],
                scalar=2.0,
                in1=m_sb[a][:, 1 : WIDTH + 1],
                op0=ALU.mult,
                op1=ALU.add,
            )

        f_ps = [psum.tile([P, WIDTH], F32, name="f%d" % a, tag="m%d" % a) for a in range(NT)]
        done = [0] * NT
        per_bank = 4 * NT

        def add_t(a, blk, src, perm):
            nc.tensor.matmul(
                out=f_ps[a][:, blk * P : (blk + 1) * P],
                lhsT=src,
                rhs=perm[:],
                is_transpose=True,
                start=(done[a] == 0),
                stop=(done[a] == per_bank - 1),
            )
            done[a] += 1

        r_sb = [epi.tile([P, WIDTH], F32, name="rsb%d" % b) for b in range(NT)]
        for b in range(NT):
            nc.scalar.copy(out=r_sb[b][:], in_=s_sb[b][:, ::-1])

        for b in range(NT):
            for a in range(NT - 1):
                add_t(a, b, t_sb[b][:, a * P + 1 : (a + 1) * P + 1], ident)
            for a in range(NT):
                add_t(a, NT - 1 - b, s_sb[b][:, a * P : (a + 1) * P], anti)
        for b in range(NT):
            a = NT - 1
            add_t(a, b, t_sb[b][:, a * P + 1 : (a + 1) * P + 1], ident)
        for a in range(NT):
            for b in range(NT):
                add_t(a, b, r_sb[b][:, a * P : (a + 1) * P], ident)
                add_t(a, NT - 1 - b, r_sb[b][:, a * P : (a + 1) * P], anti)

        for a in range(NT):
            o_sb = epi.tile([P, WIDTH], F32, name="o%d" % a)
            pieces = 2 if a == NT - 1 else 1
            step = WIDTH // pieces
            for h in range(pieces):
                cols = slice(h * step, (h + 1) * step)
                nc.vector.tensor_tensor(
                    out=o_sb[:, cols], in0=f_ps[a][:, cols], in1=dirs[a][:, cols], op=ALU.add
                )
                nc.sync.dma_start(out=out[a * P : (a + 1) * P, cols], in_=o_sb[:, cols])
